import numpy as np
import ml_dtypes


def mxq(x, axis, fmt="e4m3"):
    dtype, down = {"e4m3": (ml_dtypes.float8_e4m3fn, 7), "e5m2": (ml_dtypes.float8_e5m2, 14)}[fmt]
    v = np.moveaxis(np.asarray(x, np.float32).astype(ml_dtypes.bfloat16).astype(np.float64), axis, -1)
    blocks = v.reshape(v.shape[:-1] + (-1, 32))
    amax = np.abs(blocks).max(-1, keepdims=True)
    byte = np.maximum(np.where(amax > 0, np.frexp(amax)[1] - 1 + 127, 0) - down, 1)
    scale = np.exp2(byte - 127.0)
    codes = (blocks / scale).astype(np.float32).astype(dtype).astype(np.float64)
    return np.moveaxis((codes * scale).reshape(v.shape), -1, axis)


WIDE = False


def mx_kscale(k):
    if not WIDE:
        return np.ones(k)
    levels = np.array([10, -10, 5, -5, 0])
    a = np.random.permutation(np.resize(levels, k // 512 * 4)).reshape(k // 512, 4)
    idx = np.arange(k)
    return np.exp2(a[idx // 512, idx % 128 // 32])


BF16 = ml_dtypes.bfloat16


def bf(x):
    return np.asarray(x, np.float32).astype(BF16)


def f64(x):
    return np.asarray(x).astype(np.float64)


N, H, S, R, T = 4096, 512, 4, 128, 128


def setup_inputs():
    s = mx_kscale(H)
    return {"encodings": bf(np.random.standard_normal((N, H)) * s),
            "domain_encs": bf(np.random.standard_normal((S, H)) * s),
            "Us": bf(np.random.standard_normal((S, H, R)) / np.sqrt(H) / s[None, :, None])}


def reference(encodings, domain_encs, Us):
    diff = f64(encodings)[None, :, :] - f64(domain_encs)[:, None, :]
    proj = mxq(diff, 2, "e4m3") @ mxq(f64(Us), 1, "e4m3")
    dist = np.sqrt(np.sum(proj * proj, axis=-1))
    z = -dist
    e = np.exp(z - z.max(axis=0, keepdims=True))
    return e / e.sum(axis=0, keepdims=True)

@@ -1,0 +1,204 @@
+from contextlib import ExitStack
+
+import concourse.mybir as mybir
+from concourse.masks import make_identity
+
+F32 = mybir.dt.float32
+BF16 = mybir.dt.bfloat16
+U32 = mybir.dt.uint32
+U8 = mybir.dt.uint8
+I32 = mybir.dt.int32
+FP8X4 = mybir.dt.float8_e4m3fn_x4
+ALU = mybir.AluOpType
+ACT = mybir.ActivationFunctionType
+AX = mybir.AxisListType
+
+P = 128
+N_TOK, H, S, R = 4096, 512, 4, 128
+NT = N_TOK // P
+REP = 32
+UNITS = [1, 1] + [2] * 14 + [1, 1]
+LOADS = [1, 1, 2, 4, 8, 16]
+U_AFTER = 2
+
+FLOPS = 2 * S * N_TOK * H * R
+
+
+def tile_moe_pa_kernel(tc, encodings, domain_encs, Us, out):
+    nc = tc.nc
+    assert sum(UNITS) == NT and sum(LOADS) == NT
+    starts = [sum(UNITS[:b]) for b in range(len(UNITS))]
+    nu = len(UNITS)
+
+    with ExitStack() as ctx:
+        keep = ctx.enter_context(tc.tile_pool(name="keep", bufs=1))
+        work = ctx.enter_context(tc.tile_pool(name="work", bufs=3))
+        mxp = ctx.enter_context(tc.tile_pool(name="mxp", bufs=4))
+        ps_t = ctx.enter_context(tc.psum_pool(name="ps_t", bufs=3))
+        ps_m = ctx.enter_context(tc.psum_pool(name="ps_m", bufs=4))
+        ctx.enter_context(tc.manual_schedule())
+
+        one = keep.tile([P, 1], F32)
+        nc.vector.memset(one[:], 1.0)
+        dsrc = keep.tile([P, H], BF16)
+        nc.vector.memset(dsrc[:].bitcast(I32), 0)
+        warm = keep.tile([P, 1], F32)
+        nc.scalar.activation(out=warm[:], in_=one[:], func=ACT.Sqrt)
+        ident = keep.tile([P, P], F32)
+        make_identity(nc, ident[:])
+
+        x_all = keep.tile([P, NT, H], BF16)
+        enc_v = encodings.rearrange("(p j) h -> p j h", j=NT)
+        uraw = keep.tile([P, S * 4 * R], BF16)
+
+        nc.sync.dma_start(out=dsrc[0:S, :], in_=domain_encs)
+        j0 = 0
+        for i, cnt in enumerate(LOADS):
+            if i == U_AFTER:
+                nc.sync.dma_start(
+                    out=uraw[:].rearrange("p (a w) -> p a w", w=2 * R),
+                    in_=Us.rearrange("s (u p e) r -> p (s u) (e r)", u=2, p=P, e=2),
+                )
+            nc.sync.dma_start(out=x_all[:, j0 : j0 + cnt, :], in_=enc_v[:, j0 : j0 + cnt, :])
+            j0 += cnt
+
+        dps = ps_t.tile([P, 2, P], F32, tag="tp")
+        for u in range(2):
+            nc.tensor.transpose(dps[:, u, :], dsrc[:].bitcast(F32)[:, u * P : (u + 1) * P], ident[:])
+        domrep = keep.tile([P, S, REP * 4], BF16)
+        nc.vector.tensor_copy(
+            out=domrep[:].bitcast(F32).rearrange("p s (r u) -> p s r u", u=2),
+            in_=dps[:, :, 0:S].rearrange("p u s -> p s u").unsqueeze(2).to_broadcast([P, S, REP, 2]),
+        )
+
+        ugr = keep.tile([P, S * R * 4], BF16, align_bytes=64)
+        ucodes = keep.tile([P, S * R], U32, align_bytes=64)
+        uscl = keep.tile([P, S * R], U8, align_bytes=64)
+        d2 = keep.tile([P, S, NT], F32)
+
+        tps = {}
+        ets = {}
+        dts = {}
+        cds = {}
+        scs = {}
+
+        def stage_t(b):
+            c = UNITS[b]
+            tp = ps_t.tile([P, c, 2, P], F32, tag="tp")
+            for i in range(c):
+                xw = x_all[:, starts[b] + i, :].bitcast(F32)
+                for u in range(2):
+                    nc.tensor.transpose(tp[:, i, u, :], xw[:, u * P : (u + 1) * P], ident[:])
+            tps[b] = tp
+
+        def stage_c(b):
+            c = UNITS[b]
+            et = work.tile([P, c * P * 4], BF16, tag="et")
+            nc.scalar.copy(
+                out=et[:].bitcast(F32).rearrange("p (c n u) -> p c n u", c=c, u=2),
+                in_=tps[b][:].rearrange("p c u n -> p c n u"),
+            )
+            ets[b] = et
+
+        def stage_d(b):
+            c = UNITS[b]
+            g = c * P // REP
+            w = REP * 4
+            dt = work.tile([P, S, c * P * 4], BF16, tag="dt", align_bytes=64)
+            nc.vector.tensor_tensor(
+                out=dt[:].rearrange("p s (g w) -> p s g w", w=w),
+                in0=ets[b][:].rearrange("p (g w) -> p g w", w=w).unsqueeze(1).to_broadcast([P, S, g, w]),
+                in1=domrep[:].unsqueeze(2).to_broadcast([P, S, g, w]),
+                op=ALU.subtract,
+            )
+            dts[b] = dt
+
+        def stage_q(b):
+            c = UNITS[b]
+            cd = mxp.tile([P, S * c * P], U32, tag="cd", align_bytes=64)
+            sc = mxp.tile([P, S * c * P], U8, tag="sc", align_bytes=64)
+            nc.vector.quantize_mx(
+                out=cd[:].bitcast(FP8X4),
+                scales=sc[:],
+                in_=dts[b][:].rearrange("p s w -> p (s w)"),
+            )
+            cds[b] = cd
+            scs[b] = sc
+
+        def stage_m_s(b):
+            c = UNITS[b]
+            pjs = []
+            for i in range(c):
+                pj = ps_m.tile([P, S * R], F32, tag="pj")
+                for s in range(S):
+                    col = (s * c + i) * P
+                    nc.tensor.matmul_mx(
+                        out=pj[:, s * R : (s + 1) * R],
+                        lhsT=cds[b][:, col : col + P].bitcast(FP8X4),
+                        lhsT_scale=scs[b][:, col : col + P],
+                        rhs=ucodes[:, s * R : (s + 1) * R].bitcast(FP8X4),
+                        rhs_scale=uscl[:, s * R : (s + 1) * R],
+                        start=True,
+                        stop=True,
+                    )
+                pjs.append(pj)
+            return pjs
+
+        def stage_s(b, pjs):
+            for i, pj in enumerate(pjs):
+                j = starts[b] + i
+                for s in range(S):
+                    junk = work.tile([P, R], BF16, tag="junk")
+                    nc.scalar.activation(
+                        out=junk[:],
+                        in_=pj[:, s * R : (s + 1) * R],
+                        func=ACT.Square,
+                        accum_out=d2[:, s, j : j + 1],
+                    )
+
+        def u_regroup(s):
+            nc.scalar.copy(
+                out=ugr[:, s * R * 4 : (s + 1) * R * 4].rearrange("p (r t) -> p r t", t=4),
+                in_=uraw[:, s * R * 4 : (s + 1) * R * 4].rearrange("p (t r) -> p r t", t=4),
+            )
+
+        for k in range(nu + 3):
+            pjs = None
+            if k >= 3:
+                pjs = stage_m_s(k - 3)
+            if k < nu:
+                stage_t(k)
+                stage_c(k)
+            if k == 1 or k == 2:
+                u_regroup(2 * k - 2)
+                u_regroup(2 * k - 1)
+            if k < nu:
+                stage_d(k)
+            if k == 2:
+                nc.vector.quantize_mx(out=ucodes[:].bitcast(FP8X4), scales=uscl[:], in_=ugr[:])
+            if 1 <= k <= nu:
+                stage_q(k - 1)
+            if pjs is not None:
+                stage_s(k - 3, pjs)
+
+        dist = keep.tile([P, S, NT], F32)
+        nc.scalar.activation(out=dist[:], in_=d2[:], func=ACT.Sqrt, bias=1e-30)
+        warm2 = keep.tile([P, 1], F32)
+        nc.scalar.activation(out=warm2[:], in_=dist[:, 0, 0:1], func=ACT.Exp, scale=-1.0)
+        dmin = keep.tile([P, NT], F32)
+        nc.vector.tensor_reduce(out=dmin[:], in_=dist[:].rearrange("p s j -> p j s"), axis=AX.X, op=ALU.min)
+        z = keep.tile([P, S, NT], F32)
+        nc.vector.tensor_tensor(
+            out=z[:], in0=dmin[:].unsqueeze(1).to_broadcast([P, S, NT]), in1=dist[:], op=ALU.subtract
+        )
+        e = keep.tile([P, S, NT], F32)
+        nc.scalar.activation(out=e[:], in_=z[:], func=ACT.Exp)
+        esum = keep.tile([P, NT], F32)
+        nc.vector.tensor_reduce(out=esum[:], in_=e[:].rearrange("p s j -> p j s"), axis=AX.X, op=ALU.add)
+        rsum = keep.tile([P, NT], F32)
+        nc.vector.reciprocal(out=rsum[:], in_=esum[:])
+        res = keep.tile([P, S, NT], F32)
+        nc.vector.tensor_tensor(
+            out=res[:], in0=e[:], in1=rsum[:].unsqueeze(1).to_broadcast([P, S, NT]), op=ALU.mult
+        )
+        nc.sync.dma_start(out=out.rearrange("s (p j) -> p s j", j=NT), in_=res[:])

@@ -77,28 +77,18 @@ def tile_moe_pa_kernel(tc, encodings, domain_encs, Us, out):
         d2 = keep.tile([P, S, NT], F32)
 
         tps = {}
-        ets = {}
         dts = {}
         cds = {}
         scs = {}
 
         def stage_t(b):
             c = UNITS[b]
-            tp = ps_t.tile([P, c, 2, P], F32, tag="tp")
+            tp = ps_t.tile([P, c * P, 2], F32, tag="tp")
             for i in range(c):
                 xw = x_all[:, starts[b] + i, :].bitcast(F32)
                 for u in range(2):
-                    nc.tensor.transpose(tp[:, i, u, :], xw[:, u * P : (u + 1) * P], ident[:])
+                    nc.tensor.transpose(tp[:, i * P : (i + 1) * P, u], xw[:, u * P : (u + 1) * P], ident[:])
             tps[b] = tp
-
-        def stage_c(b):
-            c = UNITS[b]
-            et = work.tile([P, c * P * 4], BF16, tag="et")
-            nc.scalar.copy(
-                out=et[:].bitcast(F32).rearrange("p (c n u) -> p c n u", c=c, u=2),
-                in_=tps[b][:].rearrange("p c u n -> p c n u"),
-            )
-            ets[b] = et
 
         def stage_d(b):
             c = UNITS[b]
@@ -107,7 +97,12 @@ def tile_moe_pa_kernel(tc, encodings, domain_encs, Us, out):
             dt = work.tile([P, S, c * P * 4], BF16, tag="dt", align_bytes=64)
             nc.vector.tensor_tensor(
                 out=dt[:].rearrange("p s (g w) -> p s g w", w=w),
-                in0=ets[b][:].rearrange("p (g w) -> p g w", w=w).unsqueeze(1).to_broadcast([P, S, g, w]),
+                in0=tps[b][:]
+                .rearrange("p n u -> p (n u)")
+                .bitcast(BF16)
+                .rearrange("p (g w) -> p g w", w=w)
+                .unsqueeze(1)
+                .to_broadcast([P, S, g, w]),
                 in1=domrep[:].unsqueeze(2).to_broadcast([P, S, g, w]),
                 op=ALU.subtract,
             )
@@ -168,7 +163,6 @@ def tile_moe_pa_kernel(tc, encodings, domain_encs, Us, out):
                 pjs = stage_m_s(k - 3)
             if k < nu:
                 stage_t(k)
-                stage_c(k)
             if k == 1 or k == 2:
                 u_regroup(2 * k - 2)
                 u_regroup(2 * k - 1)

@@ -7,7 +7,6 @@ F32 = mybir.dt.float32
 BF16 = mybir.dt.bfloat16
 U32 = mybir.dt.uint32
 U8 = mybir.dt.uint8
-I32 = mybir.dt.int32
 FP8X4 = mybir.dt.float8_e4m3fn_x4
 ALU = mybir.AluOpType
 ACT = mybir.ActivationFunctionType
@@ -20,6 +19,7 @@ REP = 32
 UNITS = [1, 1] + [2] * 14 + [1, 1]
 LOADS = [1, 1, 2, 4, 8, 16]
 U_AFTER = 2
+GS = 32
 
 FLOPS = 2 * S * N_TOK * H * R
 
@@ -38,10 +38,11 @@ def tile_moe_pa_kernel(tc, encodings, domain_encs, Us, out):
         ps_m = ctx.enter_context(tc.psum_pool(name="ps_m", bufs=4))
         ctx.enter_context(tc.manual_schedule())
 
+        dsrc = keep.tile([P, H], BF16)
+        nc.gpsimd.memset(dsrc[:].bitcast(F32), 0.0)
+        nc.scalar.dma_start(out=dsrc[0:S, :], in_=domain_encs)
         one = keep.tile([P, 1], F32)
         nc.vector.memset(one[:], 1.0)
-        dsrc = keep.tile([P, H], BF16)
-        nc.vector.memset(dsrc[:].bitcast(I32), 0)
         warm = keep.tile([P, 1], F32)
         nc.scalar.activation(out=warm[:], in_=one[:], func=ACT.Sqrt)
         ident = keep.tile([P, P], F32)
@@ -51,7 +52,6 @@ def tile_moe_pa_kernel(tc, encodings, domain_encs, Us, out):
         enc_v = encodings.rearrange("(p j) h -> p j h", j=NT)
         uraw = keep.tile([P, S * 4 * R], BF16)
 
-        nc.sync.dma_start(out=dsrc[0:S, :], in_=domain_encs)
         j0 = 0
         for i, cnt in enumerate(LOADS):
             if i == U_AFTER:
@@ -92,13 +92,24 @@ def tile_moe_pa_kernel(tc, encodings, domain_encs, Us, out):
 
         def stage_d(b):
             c = UNITS[b]
-            g = c * P // REP
+            gs = GS if c == 2 else 0
+            nv = c * P - gs
+            g = nv // REP
             w = REP * 4
             dt = work.tile([P, S, c * P * 4], BF16, tag="dt", align_bytes=64)
+            bank = tps[b][:].rearrange("p n u -> p (n u)")
+            if gs:
+                eg = work.tile([P, gs * 4], BF16, tag="eg")
+                nc.vector.tensor_copy(out=eg[:].bitcast(F32), in_=bank[:, nv * 2 :])
+                nc.gpsimd.tensor_tensor(
+                    out=dt[:, :, nv * 4 :],
+                    in0=eg[:].unsqueeze(1).to_broadcast([P, S, gs * 4]),
+                    in1=domrep[:, :, 0 : gs * 4],
+                    op=ALU.subtract,
+                )
             nc.vector.tensor_tensor(
-                out=dt[:].rearrange("p s (g w) -> p s g w", w=w),
-                in0=tps[b][:]
-                .rearrange("p n u -> p (n u)")
+                out=dt[:, :, 0 : nv * 4].rearrange("p s (g w) -> p s g w", w=w),
+                in0=bank[:, 0 : nv * 2]
                 .bitcast(BF16)
                 .rearrange("p (g w) -> p g w", w=w)
                 .unsqueeze(1)

@@ -15,32 +15,40 @@ AX = mybir.AxisListType
 P = 128
 N_TOK, H, S, R = 4096, 512, 4, 128
 NT = N_TOK // P
-REP = 32
-UNITS = [1, 1] + [2] * 14 + [1, 1]
+REP = 8
+GS = 40
 LOADS = [1, 1, 2, 4, 8, 16]
 U_AFTER = 2
-GS = 32
+UNITS = [(0, 1), (1, 1), (2, 2)] + [(j, 2) for j in range(6, 30, 2)] + [(30, 1), (31, 1)]
+SC_UNIT = (4, 2)
+SC_FIRST = 4
+SC_PER_STEP = 2
+SC_QUANT = 12
+LAG = 3
 
 FLOPS = 2 * S * N_TOK * H * R
 
 
 def tile_moe_pa_kernel(tc, encodings, domain_encs, Us, out):
     nc = tc.nc
-    assert sum(UNITS) == NT and sum(LOADS) == NT
-    starts = [sum(UNITS[:b]) for b in range(len(UNITS))]
     nu = len(UNITS)
+    sc = nu
+    unit = dict(enumerate(UNITS))
+    unit[sc] = SC_UNIT
+    assert sum([c for (j, c) in UNITS]) + SC_UNIT[1] == NT and sum(LOADS) == NT
 
     with ExitStack() as ctx:
         keep = ctx.enter_context(tc.tile_pool(name="keep", bufs=1))
         work = ctx.enter_context(tc.tile_pool(name="work", bufs=3))
         mxp = ctx.enter_context(tc.tile_pool(name="mxp", bufs=4))
         ps_t = ctx.enter_context(tc.psum_pool(name="ps_t", bufs=3))
+        ps_s = ctx.enter_context(tc.psum_pool(name="ps_s", bufs=1))
         ps_m = ctx.enter_context(tc.psum_pool(name="ps_m", bufs=4))
         ctx.enter_context(tc.manual_schedule())
 
         dsrc = keep.tile([P, H], BF16)
         nc.gpsimd.memset(dsrc[:].bitcast(F32), 0.0)
-        nc.scalar.dma_start(out=dsrc[0:S, :], in_=domain_encs)
+        nc.sync.dma_start(out=dsrc[0:S, :], in_=domain_encs)
         one = keep.tile([P, 1], F32)
         nc.vector.memset(one[:], 1.0)
         warm = keep.tile([P, 1], F32)
@@ -70,41 +78,45 @@ def tile_moe_pa_kernel(tc, encodings, domain_encs, Us, out):
             out=domrep[:].bitcast(F32).rearrange("p s (r u) -> p s r u", u=2),
             in_=dps[:, :, 0:S].rearrange("p u s -> p s u").unsqueeze(2).to_broadcast([P, S, REP, 2]),
         )
+        negdom = keep.tile([P, S, 4], F32)
 
         ugr = keep.tile([P, S * R * 4], BF16, align_bytes=64)
         ucodes = keep.tile([P, S * R], U32, align_bytes=64)
         uscl = keep.tile([P, S * R], U8, align_bytes=64)
         d2 = keep.tile([P, S, NT], F32)
+        dt_sc = keep.tile([P, S, SC_UNIT[1] * P * 4], BF16, align_bytes=64)
 
         tps = {}
-        dts = {}
+        dts = {sc: dt_sc}
         cds = {}
         scs = {}
+        w = REP * 4
 
         def stage_t(b):
-            c = UNITS[b]
-            tp = ps_t.tile([P, c * P, 2], F32, tag="tp")
+            first, c = unit[b]
+            if b == sc:
+                tp = ps_s.tile([P, c * P, 2], F32, tag="ts")
+            else:
+                tp = ps_t.tile([P, c * P, 2], F32, tag="tp")
             for i in range(c):
-                xw = x_all[:, starts[b] + i, :].bitcast(F32)
+                xw = x_all[:, first + i, :].bitcast(F32)
                 for u in range(2):
                     nc.tensor.transpose(tp[:, i * P : (i + 1) * P, u], xw[:, u * P : (u + 1) * P], ident[:])
             tps[b] = tp
 
         def stage_d(b):
-            c = UNITS[b]
+            c = unit[b][1]
             gs = GS if c == 2 else 0
             nv = c * P - gs
-            g = nv // REP
-            w = REP * 4
             dt = work.tile([P, S, c * P * 4], BF16, tag="dt", align_bytes=64)
             bank = tps[b][:].rearrange("p n u -> p (n u)")
             if gs:
                 eg = work.tile([P, gs * 4], BF16, tag="eg")
                 nc.vector.tensor_copy(out=eg[:].bitcast(F32), in_=bank[:, nv * 2 :])
                 nc.gpsimd.tensor_tensor(
-                    out=dt[:, :, nv * 4 :],
-                    in0=eg[:].unsqueeze(1).to_broadcast([P, S, gs * 4]),
-                    in1=domrep[:, :, 0 : gs * 4],
+                    out=dt[:, :, nv * 4 :].rearrange("p s (g w) -> p s g w", w=w),
+                    in0=eg[:].rearrange("p (g w) -> p g w", w=w).unsqueeze(1).to_broadcast([P, S, gs // REP, w]),
+                    in1=domrep[:].unsqueeze(2).to_broadcast([P, S, gs // REP, w]),
                     op=ALU.subtract,
                 )
             nc.vector.tensor_tensor(
@@ -113,26 +125,36 @@ def tile_moe_pa_kernel(tc, encodings, domain_encs, Us, out):
                 .bitcast(BF16)
                 .rearrange("p (g w) -> p g w", w=w)
                 .unsqueeze(1)
-                .to_broadcast([P, S, g, w]),
-                in1=domrep[:].unsqueeze(2).to_broadcast([P, S, g, w]),
+                .to_broadcast([P, S, nv // REP, w]),
+                in1=domrep[:].unsqueeze(2).to_broadcast([P, S, nv // REP, w]),
                 op=ALU.subtract,
             )
             dts[b] = dt
 
+        def sc_piece(i):
+            s, t = divmod(i, 4)
+            nc.scalar.activation(
+                out=dt_sc[:, s, :].rearrange("p (n t) -> p n t", t=4)[:, :, t],
+                in_=tps[sc][:].rearrange("p n u -> p (n u)").bitcast(BF16).rearrange("p (n t) -> p n t", t=4)[:, :, t],
+                func=ACT.Identity,
+                bias=negdom[:, s, t : t + 1],
+                scale=1.0,
+            )
+
         def stage_q(b):
-            c = UNITS[b]
+            c = unit[b][1]
             cd = mxp.tile([P, S * c * P], U32, tag="cd", align_bytes=64)
-            sc = mxp.tile([P, S * c * P], U8, tag="sc", align_bytes=64)
+            sl = mxp.tile([P, S * c * P], U8, tag="sl", align_bytes=64)
             nc.vector.quantize_mx(
                 out=cd[:].bitcast(FP8X4),
-                scales=sc[:],
+                scales=sl[:],
                 in_=dts[b][:].rearrange("p s w -> p (s w)"),
             )
             cds[b] = cd
-            scs[b] = sc
+            scs[b] = sl
 
-        def stage_m_s(b):
-            c = UNITS[b]
+        def stage_m(b):
+            c = unit[b][1]
             pjs = []
             for i in range(c):
                 pj = ps_m.tile([P, S * R], F32, tag="pj")
@@ -152,7 +174,7 @@ def tile_moe_pa_kernel(tc, encodings, domain_encs, Us, out):
 
         def stage_s(b, pjs):
             for i, pj in enumerate(pjs):
-                j = starts[b] + i
+                j = unit[b][0] + i
                 for s in range(S):
                     junk = work.tile([P, R], BF16, tag="junk")
                     nc.scalar.activation(
@@ -168,12 +190,16 @@ def tile_moe_pa_kernel(tc, encodings, domain_encs, Us, out):
                 in_=uraw[:, s * R * 4 : (s + 1) * R * 4].rearrange("p (t r) -> p r t", t=4),
             )
 
-        for k in range(nu + 3):
-            pjs = None
-            if k >= 3:
-                pjs = stage_m_s(k - 3)
+        for k in range(nu + LAG):
             if k < nu:
                 stage_t(k)
+            if k == SC_FIRST - 1:
+                stage_t(sc)
+            done = []
+            if k >= LAG:
+                done.append((k - LAG, stage_m(k - LAG)))
+            if k == SC_QUANT + LAG:
+                done.append((sc, stage_m(sc)))
             if k == 1 or k == 2:
                 u_regroup(2 * k - 2)
                 u_regroup(2 * k - 1)
@@ -181,10 +207,18 @@ def tile_moe_pa_kernel(tc, encodings, domain_encs, Us, out):
                 stage_d(k)
             if k == 2:
                 nc.vector.quantize_mx(out=ucodes[:].bitcast(FP8X4), scales=uscl[:], in_=ugr[:])
+                nc.vector.tensor_scalar(
+                    out=negdom[:], in0=domrep[:, :, 0:4], scalar1=-1.0, scalar2=None, op0=ALU.mult
+                )
             if 1 <= k <= nu:
                 stage_q(k - 1)
-            if pjs is not None:
-                stage_s(k - 3, pjs)
+            if k == SC_QUANT:
+                stage_q(sc)
+            for i in range(SC_PER_STEP * (k - SC_FIRST), SC_PER_STEP * (k - SC_FIRST + 1)):
+                if 0 <= i < 4 * S:
+                    sc_piece(i)
+            for b, pjs in done:
+                stage_s(b, pjs)
 
         dist = keep.tile([P, S, NT], F32)
         nc.scalar.activation(out=dist[:], in_=d2[:], func=ACT.Sqrt, bias=1e-30)

@@ -16,7 +16,7 @@ P = 128
 N_TOK, H, S, R = 4096, 512, 4, 128
 NT = N_TOK // P
 REP = 8
-GS = 40
+GS = 48
 LOADS = [1, 1, 2, 4, 8, 16]
 U_AFTER = 2
 UNITS = [(0, 1), (1, 1), (2, 2)] + [(j, 2) for j in range(6, 30, 2)] + [(30, 1), (31, 1)]
@@ -48,7 +48,6 @@ def tile_moe_pa_kernel(tc, encodings, domain_encs, Us, out):
 
         dsrc = keep.tile([P, H], BF16)
         nc.gpsimd.memset(dsrc[:].bitcast(F32), 0.0)
-        nc.sync.dma_start(out=dsrc[0:S, :], in_=domain_encs)
         one = keep.tile([P, 1], F32)
         nc.vector.memset(one[:], 1.0)
         warm = keep.tile([P, 1], F32)
@@ -69,15 +68,10 @@ def tile_moe_pa_kernel(tc, encodings, domain_encs, Us, out):
                 )
             nc.sync.dma_start(out=x_all[:, j0 : j0 + cnt, :], in_=enc_v[:, j0 : j0 + cnt, :])
             j0 += cnt
+            if i == 0:
+                nc.sync.dma_start(out=dsrc[0:S, :], in_=domain_encs)
 
-        dps = ps_t.tile([P, 2, P], F32, tag="tp")
-        for u in range(2):
-            nc.tensor.transpose(dps[:, u, :], dsrc[:].bitcast(F32)[:, u * P : (u + 1) * P], ident[:])
         domrep = keep.tile([P, S, REP * 4], BF16)
-        nc.vector.tensor_copy(
-            out=domrep[:].bitcast(F32).rearrange("p s (r u) -> p s r u", u=2),
-            in_=dps[:, :, 0:S].rearrange("p u s -> p s u").unsqueeze(2).to_broadcast([P, S, REP, 2]),
-        )
         negdom = keep.tile([P, S, 4], F32)
 
         ugr = keep.tile([P, S * R * 4], BF16, align_bytes=64)
@@ -190,9 +184,20 @@ def tile_moe_pa_kernel(tc, encodings, domain_encs, Us, out):
                 in_=uraw[:, s * R * 4 : (s + 1) * R * 4].rearrange("p (t r) -> p r t", t=4),
             )
 
+        def domain_rows():
+            dps = ps_t.tile([P, 2, P], F32, tag="tp")
+            for u in range(2):
+                nc.tensor.transpose(dps[:, u, :], dsrc[:].bitcast(F32)[:, u * P : (u + 1) * P], ident[:])
+            nc.vector.tensor_copy(
+                out=domrep[:].bitcast(F32).rearrange("p s (r u) -> p s r u", u=2),
+                in_=dps[:, :, 0:S].rearrange("p u s -> p s u").unsqueeze(2).to_broadcast([P, S, REP, 2]),
+            )
+
         for k in range(nu + LAG):
             if k < nu:
                 stage_t(k)
+            if k == 0:
+                domain_rows()
             if k == SC_FIRST - 1:
                 stage_t(sc)
             done = []

@@ -16,7 +16,7 @@ P = 128
 N_TOK, H, S, R = 4096, 512, 4, 128
 NT = N_TOK // P
 REP = 8
-GS = 48
+GS = 40
 LOADS = [1, 1, 2, 4, 8, 16]
 U_AFTER = 2
 UNITS = [(0, 1), (1, 1), (2, 2)] + [(j, 2) for j in range(6, 30, 2)] + [(30, 1), (31, 1)]
@@ -44,10 +44,10 @@ def tile_moe_pa_kernel(tc, encodings, domain_encs, Us, out):
         ps_t = ctx.enter_context(tc.psum_pool(name="ps_t", bufs=3))
         ps_s = ctx.enter_context(tc.psum_pool(name="ps_s", bufs=1))
         ps_m = ctx.enter_context(tc.psum_pool(name="ps_m", bufs=4))
-        ctx.enter_context(tc.manual_schedule())
 
         dsrc = keep.tile([P, H], BF16)
         nc.gpsimd.memset(dsrc[:].bitcast(F32), 0.0)
+        nc.sync.dma_start(out=dsrc[0:S, :], in_=domain_encs)
         one = keep.tile([P, 1], F32)
         nc.vector.memset(one[:], 1.0)
         warm = keep.tile([P, 1], F32)
@@ -68,10 +68,15 @@ def tile_moe_pa_kernel(tc, encodings, domain_encs, Us, out):
                 )
             nc.sync.dma_start(out=x_all[:, j0 : j0 + cnt, :], in_=enc_v[:, j0 : j0 + cnt, :])
             j0 += cnt
-            if i == 0:
-                nc.sync.dma_start(out=dsrc[0:S, :], in_=domain_encs)
 
+        dps = ps_t.tile([P, 2, P], F32, tag="tp")
+        for u in range(2):
+            nc.tensor.transpose(dps[:, u, :], dsrc[:].bitcast(F32)[:, u * P : (u + 1) * P], ident[:])
         domrep = keep.tile([P, S, REP * 4], BF16)
+        nc.vector.tensor_copy(
+            out=domrep[:].bitcast(F32).rearrange("p s (r u) -> p s r u", u=2),
+            in_=dps[:, :, 0:S].rearrange("p u s -> p s u").unsqueeze(2).to_broadcast([P, S, REP, 2]),
+        )
         negdom = keep.tile([P, S, 4], F32)
 
         ugr = keep.tile([P, S * R * 4], BF16, align_bytes=64)
@@ -184,20 +189,9 @@ def tile_moe_pa_kernel(tc, encodings, domain_encs, Us, out):
                 in_=uraw[:, s * R * 4 : (s + 1) * R * 4].rearrange("p (t r) -> p r t", t=4),
             )
 
-        def domain_rows():
-            dps = ps_t.tile([P, 2, P], F32, tag="tp")
-            for u in range(2):
-                nc.tensor.transpose(dps[:, u, :], dsrc[:].bitcast(F32)[:, u * P : (u + 1) * P], ident[:])
-            nc.vector.tensor_copy(
-                out=domrep[:].bitcast(F32).rearrange("p s (r u) -> p s r u", u=2),
-                in_=dps[:, :, 0:S].rearrange("p u s -> p s u").unsqueeze(2).to_broadcast([P, S, REP, 2]),
-            )
-
         for k in range(nu + LAG):
             if k < nu:
                 stage_t(k)
-            if k == 0:
-                domain_rows()
             if k == SC_FIRST - 1:
                 stage_t(sc)
             done = []

from contextlib import ExitStack

import concourse.mybir as mybir
from concourse.masks import make_identity

F32 = mybir.dt.float32
BF16 = mybir.dt.bfloat16
U32 = mybir.dt.uint32
U8 = mybir.dt.uint8
FP8X4 = mybir.dt.float8_e4m3fn_x4
ALU = mybir.AluOpType
ACT = mybir.ActivationFunctionType
AX = mybir.AxisListType

P = 128
N_TOK, H, S, R = 4096, 512, 4, 128
NT = N_TOK // P
REP = 8
GS = 40
LOADS = [1, 1, 2, 4, 8, 16]
U_AFTER = 2
UNITS = [(0, 1), (1, 1), (2, 2)] + [(j, 2) for j in range(6, 30, 2)] + [(30, 1), (31, 1)]
SC_UNIT = (4, 2)
SC_FIRST = 4
SC_PER_STEP = 2
SC_QUANT = 12
LAG = 3

FLOPS = 2 * S * N_TOK * H * R


def tile_moe_pa_kernel(tc, encodings, domain_encs, Us, out):
    nc = tc.nc
    nu = len(UNITS)
    sc = nu
    unit = dict(enumerate(UNITS))
    unit[sc] = SC_UNIT
    assert sum([c for (j, c) in UNITS]) + SC_UNIT[1] == NT and sum(LOADS) == NT

    with ExitStack() as ctx:
        keep = ctx.enter_context(tc.tile_pool(name="keep", bufs=1))
        work = ctx.enter_context(tc.tile_pool(name="work", bufs=3))
        mxp = ctx.enter_context(tc.tile_pool(name="mxp", bufs=4))
        ps_t = ctx.enter_context(tc.psum_pool(name="ps_t", bufs=3))
        ps_s = ctx.enter_context(tc.psum_pool(name="ps_s", bufs=1))
        ps_m = ctx.enter_context(tc.psum_pool(name="ps_m", bufs=4))

        dsrc = keep.tile([P, H], BF16)
        nc.gpsimd.memset(dsrc[:].bitcast(F32), 0.0)
        nc.sync.dma_start(out=dsrc[0:S, :], in_=domain_encs)
        one = keep.tile([P, 1], F32)
        nc.vector.memset(one[:], 1.0)
        warm = keep.tile([P, 1], F32)
        nc.scalar.activation(out=warm[:], in_=one[:], func=ACT.Sqrt)
        ident = keep.tile([P, P], F32)
        make_identity(nc, ident[:])

        x_all = keep.tile([P, NT, H], BF16)
        enc_v = encodings.rearrange("(p j) h -> p j h", j=NT)
        uraw = keep.tile([P, S * 4 * R], BF16)

        j0 = 0
        for i, cnt in enumerate(LOADS):
            if i == U_AFTER:
                nc.sync.dma_start(
                    out=uraw[:].rearrange("p (a w) -> p a w", w=2 * R),
                    in_=Us.rearrange("s (u p e) r -> p (s u) (e r)", u=2, p=P, e=2),
                )
            nc.sync.dma_start(out=x_all[:, j0 : j0 + cnt, :], in_=enc_v[:, j0 : j0 + cnt, :])
            j0 += cnt

        dps = ps_t.tile([P, 2, P], F32, tag="tp")
        for u in range(2):
            nc.tensor.transpose(dps[:, u, :], dsrc[:].bitcast(F32)[:, u * P : (u + 1) * P], ident[:])
        domrep = keep.tile([P, S, REP * 4], BF16)
        nc.vector.tensor_copy(
            out=domrep[:].bitcast(F32).rearrange("p s (r u) -> p s r u", u=2),
            in_=dps[:, :, 0:S].rearrange("p u s -> p s u").unsqueeze(2).to_broadcast([P, S, REP, 2]),
        )
        negdom = keep.tile([P, S, 4], F32)

        ugr = keep.tile([P, S * R * 4], BF16, align_bytes=64)
        ucodes = keep.tile([P, S * R], U32, align_bytes=64)
        uscl = keep.tile([P, S * R], U8, align_bytes=64)
        d2 = keep.tile([P, S, NT], F32)
        dt_sc = keep.tile([P, S, SC_UNIT[1] * P * 4], BF16, align_bytes=64)

        tps = {}
        dts = {sc: dt_sc}
        cds = {}
        scs = {}
        w = REP * 4

        def stage_t(b):
            first, c = unit[b]
            if b == sc:
                tp = ps_s.tile([P, c * P, 2], F32, tag="ts")
            else:
                tp = ps_t.tile([P, c * P, 2], F32, tag="tp")
            for i in range(c):
                xw = x_all[:, first + i, :].bitcast(F32)
                for u in range(2):
                    nc.tensor.transpose(tp[:, i * P : (i + 1) * P, u], xw[:, u * P : (u + 1) * P], ident[:])
            tps[b] = tp

        def stage_d(b):
            c = unit[b][1]
            gs = GS if c == 2 else 0
            nv = c * P - gs
            dt = work.tile([P, S, c * P * 4], BF16, tag="dt", align_bytes=64)
            bank = tps[b][:].rearrange("p n u -> p (n u)")
            if gs:
                eg = work.tile([P, gs * 4], BF16, tag="eg")
                nc.vector.tensor_copy(out=eg[:].bitcast(F32), in_=bank[:, nv * 2 :])
                nc.gpsimd.tensor_tensor(
                    out=dt[:, :, nv * 4 :].rearrange("p s (g w) -> p s g w", w=w),
                    in0=eg[:].rearrange("p (g w) -> p g w", w=w).unsqueeze(1).to_broadcast([P, S, gs // REP, w]),
                    in1=domrep[:].unsqueeze(2).to_broadcast([P, S, gs // REP, w]),
                    op=ALU.subtract,
                )
            nc.vector.tensor_tensor(
                out=dt[:, :, 0 : nv * 4].rearrange("p s (g w) -> p s g w", w=w),
                in0=bank[:, 0 : nv * 2]
                .bitcast(BF16)
                .rearrange("p (g w) -> p g w", w=w)
                .unsqueeze(1)
                .to_broadcast([P, S, nv // REP, w]),
                in1=domrep[:].unsqueeze(2).to_broadcast([P, S, nv // REP, w]),
                op=ALU.subtract,
            )
            dts[b] = dt

        def sc_piece(i):
            s, t = divmod(i, 4)
            nc.scalar.activation(
                out=dt_sc[:, s, :].rearrange("p (n t) -> p n t", t=4)[:, :, t],
                in_=tps[sc][:].rearrange("p n u -> p (n u)").bitcast(BF16).rearrange("p (n t) -> p n t", t=4)[:, :, t],
                func=ACT.Identity,
                bias=negdom[:, s, t : t + 1],
                scale=1.0,
            )

        def stage_q(b):
            c = unit[b][1]
            cd = mxp.tile([P, S * c * P], U32, tag="cd", align_bytes=64)
            sl = mxp.tile([P, S * c * P], U8, tag="sl", align_bytes=64)
            nc.vector.quantize_mx(
                out=cd[:].bitcast(FP8X4),
                scales=sl[:],
                in_=dts[b][:].rearrange("p s w -> p (s w)"),
            )
            cds[b] = cd
            scs[b] = sl

        def stage_m(b):
            c = unit[b][1]
            pjs = []
            for i in range(c):
                pj = ps_m.tile([P, S * R], F32, tag="pj")
                for s in range(S):
                    col = (s * c + i) * P
                    nc.tensor.matmul_mx(
                        out=pj[:, s * R : (s + 1) * R],
                        lhsT=cds[b][:, col : col + P].bitcast(FP8X4),
                        lhsT_scale=scs[b][:, col : col + P],
                        rhs=ucodes[:, s * R : (s + 1) * R].bitcast(FP8X4),
                        rhs_scale=uscl[:, s * R : (s + 1) * R],
                        start=True,
                        stop=True,
                    )
                pjs.append(pj)
            return pjs

        def stage_s(b, pjs):
            for i, pj in enumerate(pjs):
                j = unit[b][0] + i
                for s in range(S):
                    junk = work.tile([P, R], BF16, tag="junk")
                    nc.scalar.activation(
                        out=junk[:],
                        in_=pj[:, s * R : (s + 1) * R],
                        func=ACT.Square,
                        accum_out=d2[:, s, j : j + 1],
                    )

        def u_regroup(s):
            nc.scalar.copy(
                out=ugr[:, s * R * 4 : (s + 1) * R * 4].rearrange("p (r t) -> p r t", t=4),
                in_=uraw[:, s * R * 4 : (s + 1) * R * 4].rearrange("p (t r) -> p r t", t=4),
            )

        for k in range(nu + LAG):
            if k < nu:
                stage_t(k)
            if k == SC_FIRST - 1:
                stage_t(sc)
            done = []
            if k >= LAG:
                done.append((k - LAG, stage_m(k - LAG)))
            if k == SC_QUANT + LAG:
                done.append((sc, stage_m(sc)))
            if k == 1 or k == 2:
                u_regroup(2 * k - 2)
                u_regroup(2 * k - 1)
            if k < nu:
                stage_d(k)
            if k == 2:
                nc.vector.quantize_mx(out=ucodes[:].bitcast(FP8X4), scales=uscl[:], in_=ugr[:])
                nc.vector.tensor_scalar(
                    out=negdom[:], in0=domrep[:, :, 0:4], scalar1=-1.0, scalar2=None, op0=ALU.mult
                )
            if 1 <= k <= nu:
                stage_q(k - 1)
            if k == SC_QUANT:
                stage_q(sc)
            for i in range(SC_PER_STEP * (k - SC_FIRST), SC_PER_STEP * (k - SC_FIRST + 1)):
                if 0 <= i < 4 * S:
                    sc_piece(i)
            for b, pjs in done:
                stage_s(b, pjs)

        dist = keep.tile([P, S, NT], F32)
        nc.scalar.activation(out=dist[:], in_=d2[:], func=ACT.Sqrt, bias=1e-30)
        warm2 = keep.tile([P, 1], F32)
        nc.scalar.activation(out=warm2[:], in_=dist[:, 0, 0:1], func=ACT.Exp, scale=-1.0)
        dmin = keep.tile([P, NT], F32)
        nc.vector.tensor_reduce(out=dmin[:], in_=dist[:].rearrange("p s j -> p j s"), axis=AX.X, op=ALU.min)
        z = keep.tile([P, S, NT], F32)
        nc.vector.tensor_tensor(
            out=z[:], in0=dmin[:].unsqueeze(1).to_broadcast([P, S, NT]), in1=dist[:], op=ALU.subtract
        )
        e = keep.tile([P, S, NT], F32)
        nc.scalar.activation(out=e[:], in_=z[:], func=ACT.Exp)
        esum = keep.tile([P, NT], F32)
        nc.vector.tensor_reduce(out=esum[:], in_=e[:].rearrange("p s j -> p j s"), axis=AX.X, op=ALU.add)
        rsum = keep.tile([P, NT], F32)
        nc.vector.reciprocal(out=rsum[:], in_=esum[:])
        res = keep.tile([P, S, NT], F32)
        nc.vector.tensor_tensor(
            out=res[:], in0=e[:], in1=rsum[:].unsqueeze(1).to_broadcast([P, S, NT]), op=ALU.mult
        )
        nc.sync.dma_start(out=out.rearrange("s (p j) -> p s j", j=NT), in_=res[:])
